import numpy as np
import ml_dtypes


def mxq(x, axis, fmt="e4m3"):
    dtype, down = {"e4m3": (ml_dtypes.float8_e4m3fn, 7), "e5m2": (ml_dtypes.float8_e5m2, 14)}[fmt]
    v = np.moveaxis(np.asarray(x, np.float32).astype(ml_dtypes.bfloat16).astype(np.float64), axis, -1)
    blocks = v.reshape(v.shape[:-1] + (-1, 32))
    amax = np.abs(blocks).max(-1, keepdims=True)
    byte = np.maximum(np.where(amax > 0, np.frexp(amax)[1] - 1 + 127, 0) - down, 1)
    scale = np.exp2(byte - 127.0)
    codes = (blocks / scale).astype(np.float32).astype(dtype).astype(np.float64)
    return np.moveaxis((codes * scale).reshape(v.shape), -1, axis)


WIDE = False


def mx_kscale(k):
    if not WIDE:
        return np.ones(k)
    levels = np.array([10, -10, 5, -5, 0])
    a = np.random.permutation(np.resize(levels, k // 512 * 4)).reshape(k // 512, 4)
    idx = np.arange(k)
    return np.exp2(a[idx // 512, idx % 128 // 32])


BF16 = ml_dtypes.bfloat16


def bf(x):
    return np.asarray(x, np.float32).astype(BF16)


def f64(x):
    return np.asarray(x).astype(np.float64)


E2M1 = np.array([0.0, 0.5, 1.0, 1.5, 2.0, 3.0, 4.0, 6.0, -0.0, -0.5, -1.0, -1.5, -2.0, -3.0, -4.0, -6.0])


def pack_weight(w, fmt):
    k, n = w.shape
    w = f64(bf(w)).reshape(k // 32, 32, n)
    amax = np.abs(w).max(1)
    if fmt == "e4m3":
        byte = np.frexp(amax)[1] - 1 + 127 - 7
    else:
        mant, ex = np.frexp(amax / 6.0)
        byte = np.where(mant > 0.5, ex, ex - 1) + 127
    byte = np.clip(np.where(amax > 0, byte, 1), 1, 254)
    scaled = (w * np.exp2(127.0 - byte)[:, None, :]).reshape(k, n).astype(np.float32)
    by_word = np.ascontiguousarray(scaled.reshape(k // 512, 128, 4, n).transpose(0, 1, 3, 2))
    if fmt == "e4m3":
        words = by_word.astype(ml_dtypes.float8_e4m3fn).view(np.uint8)
    else:
        c = by_word.astype(ml_dtypes.float4_e2m1fn).view(np.uint8) & 0xF
        words = c[..., 0::2] | (c[..., 1::2] << 4)
    return np.ascontiguousarray(words), np.ascontiguousarray(byte.astype(np.uint8).reshape(k // 512, 16, n))


def unpack_weight(words, scales, fmt):
    g, p, n, _ = words.shape
    if fmt == "e4m3":
        vals = np.ascontiguousarray(words).view(ml_dtypes.float8_e4m3fn).astype(np.float64)
    else:
        nib = np.empty((g, p, n, 4), np.uint8)
        nib[..., 0::2] = words & 0xF
        nib[..., 1::2] = words >> 4
        vals = E2M1[nib]
    vals = vals * np.repeat(np.exp2(scales.astype(np.float64) - 127.0), 8, axis=1)[..., None]
    return vals.transpose(0, 1, 3, 2).reshape(g * 512, n)

def pack4(w):
    words, scales = pack_weight(w, "e2m1")
    return words.reshape(words.shape[0], 128, -1), scales


def unpack4(words, scales):
    return unpack_weight(words.reshape(words.shape[0], 128, -1, 2), scales, "e2m1")


B, T, C, H, D = 1, 128, 8192, 16, 128
HD = H * D
HALF = D // 2
EPS = 1.1920928955078125e-07


def rope(u, cos, sin):
    u1, u2 = u[..., :HALF], u[..., HALF:]
    return np.concatenate([u1 * cos + u2 * sin, -u1 * sin + u2 * cos], axis=-1)


def rmsnorm(u):
    return u * (1.0 / np.sqrt(np.mean(u * u, axis=-1, keepdims=True) + EPS))


def setup_inputs():
    s = mx_kscale(C)
    ang = np.arange(T)[:, None] * 10000.0 ** (-np.arange(HALF) / HALF)
    x = bf(np.random.standard_normal((B, T, C)) * s)
    wq = np.random.standard_normal((HD, C)) / np.sqrt(C) / s[None, :]
    wk = np.random.standard_normal((HD, C)) / np.sqrt(C) / s[None, :]
    wq_words, wq_scales = pack4(wq.T)
    wk_words, wk_scales = pack4(wk.T)
    return {
        "x": x,
        "wq_words": wq_words,
        "wq_scales": wq_scales,
        "wk_words": wk_words,
        "wk_scales": wk_scales,
        "cos": bf(np.cos(ang))[None, :, None, :],
        "sin": bf(np.sin(ang))[None, :, None, :],
    }


def reference(x, wq_words, wq_scales, wk_words, wk_scales, cos, sin):
    xq = mxq(f64(x), 2, "e4m3")
    q = (xq @ unpack4(wq_words, wq_scales)).reshape(B, T, H, D)
    k = (xq @ unpack4(wk_words, wk_scales)).reshape(B, T, H, D)
    q = rmsnorm(rope(q, f64(cos), f64(sin)))
    k = rmsnorm(rope(k, f64(cos), f64(sin)))
    return q, k

@@ -1,0 +1,234 @@
+from contextlib import ExitStack
+
+import concourse.mybir as mybir
+from concourse.masks import make_identity
+
+BF16 = mybir.dt.bfloat16
+F32 = mybir.dt.float32
+I32 = mybir.dt.int32
+U8 = mybir.dt.uint8
+U32 = mybir.dt.uint32
+FP8X4 = mybir.dt.float8_e4m3fn_x4
+FP4X4 = mybir.dt.float4_e2m1fn_x4
+MULT = mybir.AluOpType.mult
+ADD = mybir.AluOpType.add
+SQUARE = mybir.ActivationFunctionType.Square
+SQRT = mybir.ActivationFunctionType.Sqrt
+
+P = 128
+TOKENS = 128
+FEATURES = 8192
+K_PASS = 4 * P
+GROUPS = FEATURES // K_PASS
+HEAD_DIM = 128
+HALF = HEAD_DIM // 2
+N_OUT = 2048
+BANK_COLS = 512
+BANKS = N_OUT // BANK_COLS
+HEADS_PER_BANK = BANK_COLS // HEAD_DIM
+EPS = 1.1920928955078125e-07
+
+X_CHUNKS = 4
+CHUNK_GROUPS = GROUPS // X_CHUNKS
+CHUNK_COLS = CHUNK_GROUPS * K_PASS
+WORDS_PER_GROUP = K_PASS // 2
+
+LOAD_GROUPS = 2
+LOADS = GROUPS // LOAD_GROUPS
+WORD_ROW_BYTES = 2 * N_OUT
+BANK_BYTES = 2 * BANK_COLS
+SCALE_DMA_GROUPS = 4
+
+FLOPS = 2 * TOKENS * FEATURES * 2 * N_OUT
+
+
+def load_scale_rows(nc, planes, scales):
+    planes_i32 = planes[:].bitcast(I32)
+    scales_i32 = scales.bitcast(I32)
+    for g in range(0, GROUPS, SCALE_DMA_GROUPS):
+        for low_quadrant in range(2):
+            for r in range(4):
+                nc.sync.dma_start(
+                    out=planes_i32[32 * low_quadrant + r : P : 64, g : g + SCALE_DMA_GROUPS, :],
+                    in_=scales_i32[
+                        g : g + SCALE_DMA_GROUPS, 4 * low_quadrant + r : 16 : 8, :
+                    ].rearrange("g q n -> q g n"),
+                )
+
+
+def load_words(nc, word_pool, words, load):
+    w_words = word_pool.tile([P, LOAD_GROUPS, WORD_ROW_BYTES], U8, align_bytes=64)
+    first = load * LOAD_GROUPS
+    nc.sync.dma_start(
+        out=w_words[:].bitcast(I32),
+        in_=words.bitcast(I32)[first : first + LOAD_GROUPS].rearrange("g p w -> p g w"),
+    )
+    return w_words
+
+
+def multiply_load(nc, acc, x_codes, x_scales, w_words, planes, load):
+    for i in range(LOAD_GROUPS):
+        g = load * LOAD_GROUPS + i
+        for bank in range(BANKS):
+            nc.tensor.matmul_mx(
+                out=acc[bank][:],
+                lhsT=x_codes[:, g, :].bitcast(FP8X4),
+                lhsT_scale=x_scales[:, g, :],
+                rhs=w_words[:, i, bank * BANK_BYTES : (bank + 1) * BANK_BYTES].bitcast(FP4X4),
+                rhs_scale=planes[:, g, bank * BANK_COLS : (bank + 1) * BANK_COLS],
+                start=(g == 0),
+                stop=(g == GROUPS - 1),
+            )
+
+
+def rotate_bank(nc, work, small, bank_acc, tables):
+    cos_sb, sin_sb, neg_sin, eps = tables
+    u = bank_acc[:].rearrange("p (h s d) -> p h s d", h=HEADS_PER_BANK, s=2)
+    spread = [P, HEADS_PER_BANK, HALF]
+    by_cos = work.tile([P, 2 * HEADS_PER_BANK, HALF], F32)
+    nc.vector.tensor_tensor(
+        out=by_cos[:],
+        in0=bank_acc[:].rearrange("p (r d) -> p r d", d=HALF),
+        in1=cos_sb[:].unsqueeze(1).to_broadcast([P, 2 * HEADS_PER_BANK, HALF]),
+        op=MULT,
+    )
+    by_sin = work.tile([P, HEADS_PER_BANK, 2, HALF], F32)
+    nc.vector.tensor_tensor(
+        out=by_sin[:, :, 0, :],
+        in0=u[:, :, 1, :],
+        in1=sin_sb[:].unsqueeze(1).to_broadcast(spread),
+        op=MULT,
+    )
+    nc.vector.tensor_tensor(
+        out=by_sin[:, :, 1, :],
+        in0=u[:, :, 0, :],
+        in1=neg_sin[:].unsqueeze(1).to_broadcast(spread),
+        op=MULT,
+    )
+    rotated = work.tile([P, HEADS_PER_BANK, HEAD_DIM], F32)
+    nc.vector.tensor_tensor(
+        out=rotated[:].rearrange("p h d -> p (h d)"),
+        in0=by_cos[:].rearrange("p r d -> p (r d)"),
+        in1=by_sin[:].rearrange("p h s d -> p (h s d)"),
+        op=ADD,
+    )
+    sum_sq = small.tile([P, HEADS_PER_BANK], F32)
+    for h in range(HEADS_PER_BANK):
+        squares = work.tile([P, HEAD_DIM], F32)
+        nc.scalar.activation(
+            out=squares[:], in_=rotated[:, h, :], func=SQUARE, accum_out=sum_sq[:, h : h + 1]
+        )
+    rms = small.tile([P, HEADS_PER_BANK], F32)
+    nc.scalar.activation(out=rms[:], in_=sum_sq[:], func=SQRT, scale=1.0 / HEAD_DIM, bias=eps[:])
+    return rotated, rms
+
+
+def normalise_bank(nc, small, result_pool, rotated, rms, out_cols):
+    inv_rms = small.tile([P, HEADS_PER_BANK], F32)
+    nc.vector.reciprocal(out=inv_rms[:], in_=rms[:])
+    result = result_pool.tile([P, HEADS_PER_BANK, HEAD_DIM], F32)
+    nc.vector.tensor_tensor(
+        out=result[:],
+        in0=rotated[:],
+        in1=inv_rms[:].unsqueeze(2).to_broadcast([P, HEADS_PER_BANK, HEAD_DIM]),
+        op=MULT,
+    )
+    nc.sync.dma_start(out=out_cols, in_=result[:].rearrange("p h d -> p (h d)"))
+
+
+def finish_projection(nc, work, small, result_pool, acc, tables, out):
+    out_rows = out.rearrange("b t h d -> (b t) (h d)")
+    waiting = None
+    for bank in range(BANKS):
+        rotated, rms = rotate_bank(nc, work, small, acc[bank], tables)
+        if waiting is not None:
+            normalise_bank(nc, small, result_pool, *waiting)
+        waiting = (rotated, rms, out_rows[:, bank * BANK_COLS : (bank + 1) * BANK_COLS])
+    normalise_bank(nc, small, result_pool, *waiting)
+
+
+def tile_selfattention_pa_k_kernel(
+    tc, x, wq_words, wq_scales, wk_words, wk_scales, cos, sin, out_0, out_1
+):
+    nc = tc.nc
+    x_rows = x.flatten_outer_dims()
+    with ExitStack() as ctx:
+        ctx.enter_context(tc.manual_schedule())
+        const = ctx.enter_context(tc.tile_pool(name="const", bufs=1))
+        x_pool = ctx.enter_context(tc.tile_pool(name="x_pool", bufs=X_CHUNKS))
+        word_pool = ctx.enter_context(tc.tile_pool(name="word_pool", bufs=LOADS))
+        work = ctx.enter_context(tc.tile_pool(name="work", bufs=2))
+        small = ctx.enter_context(tc.tile_pool(name="small", bufs=2))
+        result_pool = ctx.enter_context(tc.tile_pool(name="result_pool", bufs=2 * BANKS))
+        psum = ctx.enter_context(tc.psum_pool(name="psum", bufs=8))
+
+        identity = const.tile([P, P], F32)
+        make_identity(nc, identity[:])
+        cos_sb = const.tile([P, HALF], BF16)
+        sin_sb = const.tile([P, HALF], BF16)
+        nc.scalar.dma_start(out=cos_sb[:], in_=cos.flatten_outer_dims())
+        nc.scalar.dma_start(out=sin_sb[:], in_=sin.flatten_outer_dims())
+        x_codes = const.tile([P, GROUPS, TOKENS], U32, align_bytes=64)
+        x_scales = const.tile([P, GROUPS, TOKENS], U8, align_bytes=64)
+        q_planes = const.tile([P, GROUPS, N_OUT], U8, align_bytes=64)
+        k_planes = const.tile([P, GROUPS, N_OUT], U8, align_bytes=64)
+        nc.vector.memset(q_planes[:].bitcast(I32), 0)
+
+        x_chunks = []
+        for c in range(X_CHUNKS):
+            x_chunk = x_pool.tile([P, CHUNK_COLS], BF16)
+            nc.sync.dma_start(out=x_chunk[:], in_=x_rows[:, c * CHUNK_COLS : (c + 1) * CHUNK_COLS])
+            x_chunks.append(x_chunk)
+        load_scale_rows(nc, q_planes, wq_scales)
+        q_words = [load_words(nc, word_pool, wq_words, load) for load in range(LOADS)]
+
+        grouped_chunks = []
+        for c in range(X_CHUNKS):
+            x_words = x_chunks[c][:].bitcast(F32)
+            grouped = x_pool.tile([P, CHUNK_COLS], BF16, align_bytes=64)
+            grouped_words = grouped[:].bitcast(F32).rearrange(
+                "p (g r s) -> p g r s", g=CHUNK_GROUPS, s=2
+            )
+            for pair in range(CHUNK_GROUPS // 2):
+                xt = psum.tile([P, 2, 2, TOKENS], F32, tag="bank")
+                for i in range(2):
+                    first = (2 * pair + i) * WORDS_PER_GROUP
+                    for s in range(2):
+                        nc.tensor.transpose(
+                            xt[:, i, s, :],
+                            x_words[:, first + s : first + WORDS_PER_GROUP : 2],
+                            identity[:],
+                        )
+                copy_out = nc.vector.tensor_copy if pair == 0 else nc.scalar.copy
+                copy_out(
+                    out=grouped_words[:, 2 * pair : 2 * pair + 2],
+                    in_=xt[:].rearrange("p g s r -> p g r s"),
+                )
+            grouped_chunks.append(grouped)
+        for c in range(X_CHUNKS):
+            groups = slice(c * CHUNK_GROUPS, (c + 1) * CHUNK_GROUPS)
+            nc.vector.quantize_mx(
+                out=x_codes[:, groups, :].rearrange("p g r -> p (g r)").bitcast(FP8X4),
+                scales=x_scales[:, groups, :].rearrange("p g r -> p (g r)"),
+                in_=grouped_chunks[c][:],
+            )
+
+        nc.vector.memset(k_planes[:].bitcast(I32), 0)
+        load_scale_rows(nc, k_planes, wk_scales)
+        neg_sin = const.tile([P, HALF], BF16)
+        nc.vector.tensor_scalar_mul(out=neg_sin[:], in0=sin_sb[:], scalar1=-1.0)
+        eps = const.tile([P, 1], F32)
+        nc.vector.memset(eps[:], EPS)
+        tables = (cos_sb, sin_sb, neg_sin, eps)
+
+        q_acc = [psum.tile([P, BANK_COLS], F32, tag="bank", name="q_acc%d" % b) for b in range(BANKS)]
+        k_acc = [psum.tile([P, BANK_COLS], F32, tag="bank", name="k_acc%d" % b) for b in range(BANKS)]
+        k_words = []
+        for load in range(LOADS):
+            multiply_load(nc, q_acc, x_codes, x_scales, q_words[load], q_planes, load)
+            k_words.append(load_words(nc, word_pool, wk_words, load))
+
+        finish_projection(nc, work, small, result_pool, q_acc, tables, out_0)
+        for load in range(LOADS):
+            multiply_load(nc, k_acc, x_codes, x_scales, k_words[load], k_planes, load)
+        finish_projection(nc, work, small, result_pool, k_acc, tables, out_1)

@@ -38,6 +38,9 @@ LOADS = GROUPS // LOAD_GROUPS
 WORD_ROW_BYTES = 2 * N_OUT
 BANK_BYTES = 2 * BANK_COLS
 SCALE_DMA_GROUPS = 4
+TAIL_GROUPS = LOAD_GROUPS * BANKS
+WIDE_LOADS = (GROUPS - TAIL_GROUPS) // LOAD_GROUPS
+TAIL_DMA_GROUPS = TAIL_GROUPS // 2
 
 FLOPS = 2 * TOKENS * FEATURES * 2 * N_OUT
 
@@ -66,6 +69,18 @@ def load_words(nc, word_pool, words, load):
     return w_words
 
 
+def load_tail_words(nc, word_pool, words, bank):
+    w_words = word_pool.tile([P, TAIL_GROUPS, BANK_BYTES], U8, align_bytes=64)
+    bank_words = words.bitcast(I32)[:, :, bank * BANK_BYTES // 4 : (bank + 1) * BANK_BYTES // 4]
+    for i in range(0, TAIL_GROUPS, TAIL_DMA_GROUPS):
+        first = GROUPS - TAIL_GROUPS + i
+        nc.sync.dma_start(
+            out=w_words[:, i : i + TAIL_DMA_GROUPS, :].bitcast(I32),
+            in_=bank_words[first : first + TAIL_DMA_GROUPS].rearrange("g p w -> p g w"),
+        )
+    return w_words
+
+
 def multiply_load(nc, acc, x_codes, x_scales, w_words, planes, load):
     for i in range(LOAD_GROUPS):
         g = load * LOAD_GROUPS + i
@@ -79,6 +94,20 @@ def multiply_load(nc, acc, x_codes, x_scales, w_words, planes, load):
                 start=(g == 0),
                 stop=(g == GROUPS - 1),
             )
+
+
+def multiply_tail(nc, acc, x_codes, x_scales, w_words, planes, bank):
+    for i in range(TAIL_GROUPS):
+        g = GROUPS - TAIL_GROUPS + i
+        nc.tensor.matmul_mx(
+            out=acc[bank][:],
+            lhsT=x_codes[:, g, :].bitcast(FP8X4),
+            lhsT_scale=x_scales[:, g, :],
+            rhs=w_words[:, i, :].bitcast(FP4X4),
+            rhs_scale=planes[:, g, bank * BANK_COLS : (bank + 1) * BANK_COLS],
+            start=False,
+            stop=(g == GROUPS - 1),
+        )
 
 
 def rotate_bank(nc, work, small, bank_acc, tables):
@@ -226,9 +255,14 @@ def tile_selfattention_pa_k_kernel(
         k_words = []
         for load in range(LOADS):
             multiply_load(nc, q_acc, x_codes, x_scales, q_words[load], q_planes, load)
-            k_words.append(load_words(nc, word_pool, wk_words, load))
+            if load < WIDE_LOADS:
+                k_words.append(load_words(nc, word_pool, wk_words, load))
+            else:
+                k_words.append(load_tail_words(nc, word_pool, wk_words, load - WIDE_LOADS))
 
         finish_projection(nc, work, small, result_pool, q_acc, tables, out_0)
-        for load in range(LOADS):
+        for load in range(WIDE_LOADS):
             multiply_load(nc, k_acc, x_codes, x_scales, k_words[load], k_planes, load)
+        for bank in range(BANKS):
+            multiply_tail(nc, k_acc, x_codes, x_scales, k_words[WIDE_LOADS + bank], k_planes, bank)
         finish_projection(nc, work, small, result_pool, k_acc, tables, out_1)

@@ -13,7 +13,8 @@ FP4X4 = mybir.dt.float4_e2m1fn_x4
 MULT = mybir.AluOpType.mult
 ADD = mybir.AluOpType.add
 SQUARE = mybir.ActivationFunctionType.Square
-SQRT = mybir.ActivationFunctionType.Sqrt
+INV_SQRT = mybir.ActivationFunctionType.Abs_reciprocal_sqrt
+COPY = mybir.ActivationFunctionType.Copy
 
 P = 128
 TOKENS = 128
@@ -40,7 +41,10 @@ BANK_BYTES = 2 * BANK_COLS
 SCALE_DMA_GROUPS = 4
 TAIL_GROUPS = LOAD_GROUPS * BANKS
 WIDE_LOADS = (GROUPS - TAIL_GROUPS) // LOAD_GROUPS
-TAIL_DMA_GROUPS = TAIL_GROUPS // 2
+TAIL_DMA_GROUPS = (4, 4)
+LAST_TAIL_DMA_GROUPS = (4, 3, 1)
+
+LAST_PIECES = 2
 
 FLOPS = 2 * TOKENS * FEATURES * 2 * N_OUT
 
@@ -72,12 +76,14 @@ def load_words(nc, word_pool, words, load):
 def load_tail_words(nc, word_pool, words, bank):
     w_words = word_pool.tile([P, TAIL_GROUPS, BANK_BYTES], U8, align_bytes=64)
     bank_words = words.bitcast(I32)[:, :, bank * BANK_BYTES // 4 : (bank + 1) * BANK_BYTES // 4]
-    for i in range(0, TAIL_GROUPS, TAIL_DMA_GROUPS):
+    i = 0
+    for groups in LAST_TAIL_DMA_GROUPS if bank == BANKS - 1 else TAIL_DMA_GROUPS:
         first = GROUPS - TAIL_GROUPS + i
         nc.sync.dma_start(
-            out=w_words[:, i : i + TAIL_DMA_GROUPS, :].bitcast(I32),
-            in_=bank_words[first : first + TAIL_DMA_GROUPS].rearrange("g p w -> p g w"),
+            out=w_words[:, i : i + groups, :].bitcast(I32),
+            in_=bank_words[first : first + groups].rearrange("g p w -> p g w"),
         )
+        i += groups
     return w_words
 
 
@@ -110,18 +116,19 @@ def multiply_tail(nc, acc, x_codes, x_scales, w_words, planes, bank):
         )
 
 
-def rotate_bank(nc, work, small, bank_acc, tables):
+def finish_heads(nc, work, small, result_pool, heads_acc, tables, out_cols):
     cos_sb, sin_sb, neg_sin, eps = tables
-    u = bank_acc[:].rearrange("p (h s d) -> p h s d", h=HEADS_PER_BANK, s=2)
-    spread = [P, HEADS_PER_BANK, HALF]
-    by_cos = work.tile([P, 2 * HEADS_PER_BANK, HALF], F32)
+    heads = heads_acc.shape[1] // HEAD_DIM
+    u = heads_acc.rearrange("p (h s d) -> p h s d", h=heads, s=2)
+    spread = [P, heads, HALF]
+    by_cos = work.tile([P, 2 * heads, HALF], F32)
     nc.vector.tensor_tensor(
         out=by_cos[:],
-        in0=bank_acc[:].rearrange("p (r d) -> p r d", d=HALF),
-        in1=cos_sb[:].unsqueeze(1).to_broadcast([P, 2 * HEADS_PER_BANK, HALF]),
+        in0=heads_acc.rearrange("p (r d) -> p r d", d=HALF),
+        in1=cos_sb[:].unsqueeze(1).to_broadcast([P, 2 * heads, HALF]),
         op=MULT,
     )
-    by_sin = work.tile([P, HEADS_PER_BANK, 2, HALF], F32)
+    by_sin = work.tile([P, heads, 2, HALF], F32)
     nc.vector.tensor_tensor(
         out=by_sin[:, :, 0, :],
         in0=u[:, :, 1, :],
@@ -134,46 +141,47 @@ def rotate_bank(nc, work, small, bank_acc, tables):
         in1=neg_sin[:].unsqueeze(1).to_broadcast(spread),
         op=MULT,
     )
-    rotated = work.tile([P, HEADS_PER_BANK, HEAD_DIM], F32)
+    rotated = work.tile([P, heads, HEAD_DIM], F32)
     nc.vector.tensor_tensor(
         out=rotated[:].rearrange("p h d -> p (h d)"),
         in0=by_cos[:].rearrange("p r d -> p (r d)"),
         in1=by_sin[:].rearrange("p h s d -> p (h s d)"),
         op=ADD,
     )
-    sum_sq = small.tile([P, HEADS_PER_BANK], F32)
-    for h in range(HEADS_PER_BANK):
+    sum_sq = small.tile([P, heads], F32)
+    for h in range(heads):
         squares = work.tile([P, HEAD_DIM], F32)
         nc.scalar.activation(
             out=squares[:], in_=rotated[:, h, :], func=SQUARE, accum_out=sum_sq[:, h : h + 1]
         )
-    rms = small.tile([P, HEADS_PER_BANK], F32)
-    nc.scalar.activation(out=rms[:], in_=sum_sq[:], func=SQRT, scale=1.0 / HEAD_DIM, bias=eps[:])
-    return rotated, rms
-
-
-def normalise_bank(nc, small, result_pool, rotated, rms, out_cols):
-    inv_rms = small.tile([P, HEADS_PER_BANK], F32)
-    nc.vector.reciprocal(out=inv_rms[:], in_=rms[:])
-    result = result_pool.tile([P, HEADS_PER_BANK, HEAD_DIM], F32)
-    nc.vector.tensor_tensor(
-        out=result[:],
-        in0=rotated[:],
-        in1=inv_rms[:].unsqueeze(2).to_broadcast([P, HEADS_PER_BANK, HEAD_DIM]),
-        op=MULT,
+    inv_rms = small.tile([P, heads], F32)
+    nc.scalar.activation(
+        out=inv_rms[:], in_=sum_sq[:], func=INV_SQRT, scale=1.0 / HEAD_DIM, bias=eps[:]
     )
+    result = result_pool.tile([P, heads, HEAD_DIM], F32)
+    for h in range(heads):
+        nc.scalar.activation(
+            out=result[:, h, :], in_=rotated[:, h, :], func=COPY, scale=inv_rms[:, h : h + 1]
+        )
     nc.sync.dma_start(out=out_cols, in_=result[:].rearrange("p h d -> p (h d)"))
 
 
-def finish_projection(nc, work, small, result_pool, acc, tables, out):
+def finish_projection(nc, work, small, result_pool, acc, tables, out, last_bank_pieces):
     out_rows = out.rearrange("b t h d -> (b t) (h d)")
-    waiting = None
     for bank in range(BANKS):
-        rotated, rms = rotate_bank(nc, work, small, acc[bank], tables)
-        if waiting is not None:
-            normalise_bank(nc, small, result_pool, *waiting)
-        waiting = (rotated, rms, out_rows[:, bank * BANK_COLS : (bank + 1) * BANK_COLS])
-    normalise_bank(nc, small, result_pool, *waiting)
+        pieces = last_bank_pieces if bank == BANKS - 1 else 1
+        piece_cols = BANK_COLS // pieces
+        for piece in range(pieces):
+            first = piece * piece_cols
+            finish_heads(
+                nc,
+                work,
+                small,
+                result_pool,
+                acc[bank][:, first : first + piece_cols],
+                tables,
+                out_rows[:, bank * BANK_COLS + first : bank * BANK_COLS + first + piece_cols],
+            )
 
 
 def tile_selfattention_pa_k_kernel(
@@ -188,7 +196,7 @@ def tile_selfattention_pa_k_kernel(
         word_pool = ctx.enter_context(tc.tile_pool(name="word_pool", bufs=LOADS))
         work = ctx.enter_context(tc.tile_pool(name="work", bufs=2))
         small = ctx.enter_context(tc.tile_pool(name="small", bufs=2))
-        result_pool = ctx.enter_context(tc.tile_pool(name="result_pool", bufs=2 * BANKS))
+        result_pool = ctx.enter_context(tc.tile_pool(name="result_pool", bufs=2 * BANKS - 1 + LAST_PIECES))
         psum = ctx.enter_context(tc.psum_pool(name="psum", bufs=8))
 
         identity = const.tile([P, P], F32)
@@ -260,9 +268,9 @@ def tile_selfattention_pa_k_kernel(
             else:
                 k_words.append(load_tail_words(nc, word_pool, wk_words, load - WIDE_LOADS))
 
-        finish_projection(nc, work, small, result_pool, q_acc, tables, out_0)
+        finish_projection(nc, work, small, result_pool, q_acc, tables, out_0, 1)
         for load in range(WIDE_LOADS):
             multiply_load(nc, k_acc, x_codes, x_scales, k_words[load], k_planes, load)
         for bank in range(BANKS):
             multiply_tail(nc, k_acc, x_codes, x_scales, k_words[WIDE_LOADS + bank], k_planes, bank)
-        finish_projection(nc, work, small, result_pool, k_acc, tables, out_1)
+        finish_projection(nc, work, small, result_pool, k_acc, tables, out_1, LAST_PIECES)

@@ -39,6 +39,8 @@ LOADS = GROUPS // LOAD_GROUPS
 WORD_ROW_BYTES = 2 * N_OUT
 BANK_BYTES = 2 * BANK_COLS
 SCALE_DMA_GROUPS = 4
+RUN_GROUPS = GROUPS // 2
+RUN_LOADS = RUN_GROUPS // LOAD_GROUPS
 TAIL_GROUPS = LOAD_GROUPS * BANKS
 WIDE_LOADS = (GROUPS - TAIL_GROUPS) // LOAD_GROUPS
 TAIL_DMA_GROUPS = (4, 4)
@@ -49,10 +51,10 @@ LAST_PIECES = 2
 FLOPS = 2 * TOKENS * FEATURES * 2 * N_OUT
 
 
-def load_scale_rows(nc, planes, scales):
+def load_scale_rows(nc, planes, scales, run):
     planes_i32 = planes[:].bitcast(I32)
     scales_i32 = scales.bitcast(I32)
-    for g in range(0, GROUPS, SCALE_DMA_GROUPS):
+    for g in range(run * RUN_GROUPS, (run + 1) * RUN_GROUPS, SCALE_DMA_GROUPS):
         for low_quadrant in range(2):
             for r in range(4):
                 nc.sync.dma_start(
@@ -216,8 +218,11 @@ def tile_selfattention_pa_k_kernel(
             x_chunk = x_pool.tile([P, CHUNK_COLS], BF16)
             nc.sync.dma_start(out=x_chunk[:], in_=x_rows[:, c * CHUNK_COLS : (c + 1) * CHUNK_COLS])
             x_chunks.append(x_chunk)
-        load_scale_rows(nc, q_planes, wq_scales)
-        q_words = [load_words(nc, word_pool, wq_words, load) for load in range(LOADS)]
+        q_words = []
+        for load in range(LOADS):
+            if load % RUN_LOADS == 0:
+                load_scale_rows(nc, q_planes, wq_scales, load // RUN_LOADS)
+            q_words.append(load_words(nc, word_pool, wq_words, load))
 
         grouped_chunks = []
         for c in range(X_CHUNKS):
@@ -251,7 +256,7 @@ def tile_selfattention_pa_k_kernel(
             )
 
         nc.vector.memset(k_planes[:].bitcast(I32), 0)
-        load_scale_rows(nc, k_planes, wk_scales)
+        load_scale_rows(nc, k_planes, wk_scales, 0)
         neg_sin = const.tile([P, HALF], BF16)
         nc.vector.tensor_scalar_mul(out=neg_sin[:], in0=sin_sb[:], scalar1=-1.0)
         eps = const.tile([P, 1], F32)
@@ -266,6 +271,8 @@ def tile_selfattention_pa_k_kernel(
             if load < WIDE_LOADS:
                 k_words.append(load_words(nc, word_pool, wk_words, load))
             else:
+                if load == WIDE_LOADS:
+                    load_scale_rows(nc, k_planes, wk_scales, 1)
                 k_words.append(load_tail_words(nc, word_pool, wk_words, load - WIDE_LOADS))
 
         finish_projection(nc, work, small, result_pool, q_acc, tables, out_0, 1)

@@ -39,7 +39,8 @@ LOADS = GROUPS // LOAD_GROUPS
 WORD_ROW_BYTES = 2 * N_OUT
 BANK_BYTES = 2 * BANK_COLS
 SCALE_DMA_GROUPS = 4
-RUN_GROUPS = GROUPS // 2
+RUNS = 2
+RUN_GROUPS = GROUPS // RUNS
 RUN_LOADS = RUN_GROUPS // LOAD_GROUPS
 TAIL_GROUPS = LOAD_GROUPS * BANKS
 WIDE_LOADS = (GROUPS - TAIL_GROUPS) // LOAD_GROUPS
@@ -52,13 +53,14 @@ FLOPS = 2 * TOKENS * FEATURES * 2 * N_OUT
 
 
 def load_scale_rows(nc, planes, scales, run):
-    planes_i32 = planes[:].bitcast(I32)
+    planes_i32 = planes[run][:].bitcast(I32)
     scales_i32 = scales.bitcast(I32)
-    for g in range(run * RUN_GROUPS, (run + 1) * RUN_GROUPS, SCALE_DMA_GROUPS):
+    for i in range(0, RUN_GROUPS, SCALE_DMA_GROUPS):
+        g = run * RUN_GROUPS + i
         for low_quadrant in range(2):
             for r in range(4):
                 nc.sync.dma_start(
-                    out=planes_i32[32 * low_quadrant + r : P : 64, g : g + SCALE_DMA_GROUPS, :],
+                    out=planes_i32[32 * low_quadrant + r : P : 64, i : i + SCALE_DMA_GROUPS, :],
                     in_=scales_i32[
                         g : g + SCALE_DMA_GROUPS, 4 * low_quadrant + r : 16 : 8, :
                     ].rearrange("g q n -> q g n"),
@@ -89,6 +91,10 @@ def load_tail_words(nc, word_pool, words, bank):
     return w_words
 
 
+def plane_of(planes, g, bank):
+    return planes[g // RUN_GROUPS][:, g % RUN_GROUPS, bank * BANK_COLS : (bank + 1) * BANK_COLS]
+
+
 def multiply_load(nc, acc, x_codes, x_scales, w_words, planes, load):
     for i in range(LOAD_GROUPS):
         g = load * LOAD_GROUPS + i
@@ -98,7 +104,7 @@ def multiply_load(nc, acc, x_codes, x_scales, w_words, planes, load):
                 lhsT=x_codes[:, g, :].bitcast(FP8X4),
                 lhsT_scale=x_scales[:, g, :],
                 rhs=w_words[:, i, bank * BANK_BYTES : (bank + 1) * BANK_BYTES].bitcast(FP4X4),
-                rhs_scale=planes[:, g, bank * BANK_COLS : (bank + 1) * BANK_COLS],
+                rhs_scale=plane_of(planes, g, bank),
                 start=(g == 0),
                 stop=(g == GROUPS - 1),
             )
@@ -112,7 +118,7 @@ def multiply_tail(nc, acc, x_codes, x_scales, w_words, planes, bank):
             lhsT=x_codes[:, g, :].bitcast(FP8X4),
             lhsT_scale=x_scales[:, g, :],
             rhs=w_words[:, i, :].bitcast(FP4X4),
-            rhs_scale=planes[:, g, bank * BANK_COLS : (bank + 1) * BANK_COLS],
+            rhs_scale=plane_of(planes, g, bank),
             start=False,
             stop=(g == GROUPS - 1),
         )
@@ -209,9 +215,16 @@ def tile_selfattention_pa_k_kernel(
         nc.scalar.dma_start(out=sin_sb[:], in_=sin.flatten_outer_dims())
         x_codes = const.tile([P, GROUPS, TOKENS], U32, align_bytes=64)
         x_scales = const.tile([P, GROUPS, TOKENS], U8, align_bytes=64)
-        q_planes = const.tile([P, GROUPS, N_OUT], U8, align_bytes=64)
-        k_planes = const.tile([P, GROUPS, N_OUT], U8, align_bytes=64)
-        nc.vector.memset(q_planes[:].bitcast(I32), 0)
+        q_planes = [
+            const.tile([P, RUN_GROUPS, N_OUT], U8, align_bytes=64, name="q_planes%d" % run)
+            for run in range(RUNS)
+        ]
+        k_planes = [
+            const.tile([P, RUN_GROUPS, N_OUT], U8, align_bytes=64, name="k_planes%d" % run)
+            for run in range(RUNS)
+        ]
+        for run in range(RUNS):
+            nc.vector.memset(q_planes[run][:].bitcast(I32), 0)
 
         x_chunks = []
         for c in range(X_CHUNKS):
@@ -255,7 +268,8 @@ def tile_selfattention_pa_k_kernel(
                 in_=grouped_chunks[c][:],
             )
 
-        nc.vector.memset(k_planes[:].bitcast(I32), 0)
+        for run in range(RUNS):
+            nc.vector.memset(k_planes[run][:].bitcast(I32), 0)
         load_scale_rows(nc, k_planes, wk_scales, 0)
         neg_sin = const.tile([P, HALF], BF16)
         nc.vector.tensor_scalar_mul(out=neg_sin[:], in0=sin_sb[:], scalar1=-1.0)

@@ -231,11 +231,9 @@ def tile_selfattention_pa_k_kernel(
             x_chunk = x_pool.tile([P, CHUNK_COLS], BF16)
             nc.sync.dma_start(out=x_chunk[:], in_=x_rows[:, c * CHUNK_COLS : (c + 1) * CHUNK_COLS])
             x_chunks.append(x_chunk)
-        q_words = []
-        for load in range(LOADS):
-            if load % RUN_LOADS == 0:
-                load_scale_rows(nc, q_planes, wq_scales, load // RUN_LOADS)
-            q_words.append(load_words(nc, word_pool, wq_words, load))
+        for run in range(RUNS):
+            load_scale_rows(nc, q_planes, wq_scales, run)
+        q_words = [load_words(nc, word_pool, wq_words, load) for load in range(LOADS)]
 
         grouped_chunks = []
         for c in range(X_CHUNKS):

@@ -225,6 +225,7 @@ def tile_selfattention_pa_k_kernel(
         ]
         for run in range(RUNS):
             nc.vector.memset(q_planes[run][:].bitcast(I32), 0)
+        nc.vector.memset(k_planes[0][:].bitcast(I32), 0)
 
         x_chunks = []
         for c in range(X_CHUNKS):
@@ -233,6 +234,7 @@ def tile_selfattention_pa_k_kernel(
             x_chunks.append(x_chunk)
         for run in range(RUNS):
             load_scale_rows(nc, q_planes, wq_scales, run)
+        load_scale_rows(nc, k_planes, wk_scales, 0)
         q_words = [load_words(nc, word_pool, wq_words, load) for load in range(LOADS)]
 
         grouped_chunks = []
@@ -266,9 +268,7 @@ def tile_selfattention_pa_k_kernel(
                 in_=grouped_chunks[c][:],
             )
 
-        for run in range(RUNS):
-            nc.vector.memset(k_planes[run][:].bitcast(I32), 0)
-        load_scale_rows(nc, k_planes, wk_scales, 0)
+        nc.vector.memset(k_planes[1][:].bitcast(I32), 0)
         neg_sin = const.tile([P, HALF], BF16)
         nc.vector.tensor_scalar_mul(out=neg_sin[:], in0=sin_sb[:], scalar1=-1.0)
         eps = const.tile([P, 1], F32)

@@ -57,8 +57,8 @@ def load_scale_rows(nc, planes, scales, run):
     scales_i32 = scales.bitcast(I32)
     for i in range(0, RUN_GROUPS, SCALE_DMA_GROUPS):
         g = run * RUN_GROUPS + i
-        for low_quadrant in range(2):
-            for r in range(4):
+        for r in range(4):
+            for low_quadrant in range(2):
                 nc.sync.dma_start(
                     out=planes_i32[32 * low_quadrant + r : P : 64, i : i + SCALE_DMA_GROUPS, :],
                     in_=scales_i32[

from contextlib import ExitStack

import concourse.mybir as mybir
from concourse.masks import make_identity

BF16 = mybir.dt.bfloat16
F32 = mybir.dt.float32
I32 = mybir.dt.int32
U8 = mybir.dt.uint8
U32 = mybir.dt.uint32
FP8X4 = mybir.dt.float8_e4m3fn_x4
FP4X4 = mybir.dt.float4_e2m1fn_x4
MULT = mybir.AluOpType.mult
ADD = mybir.AluOpType.add
SQUARE = mybir.ActivationFunctionType.Square
INV_SQRT = mybir.ActivationFunctionType.Abs_reciprocal_sqrt
COPY = mybir.ActivationFunctionType.Copy

P = 128
TOKENS = 128
FEATURES = 8192
K_PASS = 4 * P
GROUPS = FEATURES // K_PASS
HEAD_DIM = 128
HALF = HEAD_DIM // 2
N_OUT = 2048
BANK_COLS = 512
BANKS = N_OUT // BANK_COLS
HEADS_PER_BANK = BANK_COLS // HEAD_DIM
EPS = 1.1920928955078125e-07

X_CHUNKS = 4
CHUNK_GROUPS = GROUPS // X_CHUNKS
CHUNK_COLS = CHUNK_GROUPS * K_PASS
WORDS_PER_GROUP = K_PASS // 2

LOAD_GROUPS = 2
LOADS = GROUPS // LOAD_GROUPS
WORD_ROW_BYTES = 2 * N_OUT
BANK_BYTES = 2 * BANK_COLS
SCALE_DMA_GROUPS = 4
RUNS = 2
RUN_GROUPS = GROUPS // RUNS
RUN_LOADS = RUN_GROUPS // LOAD_GROUPS
TAIL_GROUPS = LOAD_GROUPS * BANKS
WIDE_LOADS = (GROUPS - TAIL_GROUPS) // LOAD_GROUPS
TAIL_DMA_GROUPS = (4, 4)
LAST_TAIL_DMA_GROUPS = (4, 3, 1)

LAST_PIECES = 2

FLOPS = 2 * TOKENS * FEATURES * 2 * N_OUT


def load_scale_rows(nc, planes, scales, run):
    planes_i32 = planes[run][:].bitcast(I32)
    scales_i32 = scales.bitcast(I32)
    for i in range(0, RUN_GROUPS, SCALE_DMA_GROUPS):
        g = run * RUN_GROUPS + i
        for r in range(4):
            for low_quadrant in range(2):
                nc.sync.dma_start(
                    out=planes_i32[32 * low_quadrant + r : P : 64, i : i + SCALE_DMA_GROUPS, :],
                    in_=scales_i32[
                        g : g + SCALE_DMA_GROUPS, 4 * low_quadrant + r : 16 : 8, :
                    ].rearrange("g q n -> q g n"),
                )


def load_words(nc, word_pool, words, load):
    w_words = word_pool.tile([P, LOAD_GROUPS, WORD_ROW_BYTES], U8, align_bytes=64)
    first = load * LOAD_GROUPS
    nc.sync.dma_start(
        out=w_words[:].bitcast(I32),
        in_=words.bitcast(I32)[first : first + LOAD_GROUPS].rearrange("g p w -> p g w"),
    )
    return w_words


def load_tail_words(nc, word_pool, words, bank):
    w_words = word_pool.tile([P, TAIL_GROUPS, BANK_BYTES], U8, align_bytes=64)
    bank_words = words.bitcast(I32)[:, :, bank * BANK_BYTES // 4 : (bank + 1) * BANK_BYTES // 4]
    i = 0
    for groups in LAST_TAIL_DMA_GROUPS if bank == BANKS - 1 else TAIL_DMA_GROUPS:
        first = GROUPS - TAIL_GROUPS + i
        nc.sync.dma_start(
            out=w_words[:, i : i + groups, :].bitcast(I32),
            in_=bank_words[first : first + groups].rearrange("g p w -> p g w"),
        )
        i += groups
    return w_words


def plane_of(planes, g, bank):
    return planes[g // RUN_GROUPS][:, g % RUN_GROUPS, bank * BANK_COLS : (bank + 1) * BANK_COLS]


def multiply_load(nc, acc, x_codes, x_scales, w_words, planes, load):
    for i in range(LOAD_GROUPS):
        g = load * LOAD_GROUPS + i
        for bank in range(BANKS):
            nc.tensor.matmul_mx(
                out=acc[bank][:],
                lhsT=x_codes[:, g, :].bitcast(FP8X4),
                lhsT_scale=x_scales[:, g, :],
                rhs=w_words[:, i, bank * BANK_BYTES : (bank + 1) * BANK_BYTES].bitcast(FP4X4),
                rhs_scale=plane_of(planes, g, bank),
                start=(g == 0),
                stop=(g == GROUPS - 1),
            )


def multiply_tail(nc, acc, x_codes, x_scales, w_words, planes, bank):
    for i in range(TAIL_GROUPS):
        g = GROUPS - TAIL_GROUPS + i
        nc.tensor.matmul_mx(
            out=acc[bank][:],
            lhsT=x_codes[:, g, :].bitcast(FP8X4),
            lhsT_scale=x_scales[:, g, :],
            rhs=w_words[:, i, :].bitcast(FP4X4),
            rhs_scale=plane_of(planes, g, bank),
            start=False,
            stop=(g == GROUPS - 1),
        )


def finish_heads(nc, work, small, result_pool, heads_acc, tables, out_cols):
    cos_sb, sin_sb, neg_sin, eps = tables
    heads = heads_acc.shape[1] // HEAD_DIM
    u = heads_acc.rearrange("p (h s d) -> p h s d", h=heads, s=2)
    spread = [P, heads, HALF]
    by_cos = work.tile([P, 2 * heads, HALF], F32)
    nc.vector.tensor_tensor(
        out=by_cos[:],
        in0=heads_acc.rearrange("p (r d) -> p r d", d=HALF),
        in1=cos_sb[:].unsqueeze(1).to_broadcast([P, 2 * heads, HALF]),
        op=MULT,
    )
    by_sin = work.tile([P, heads, 2, HALF], F32)
    nc.vector.tensor_tensor(
        out=by_sin[:, :, 0, :],
        in0=u[:, :, 1, :],
        in1=sin_sb[:].unsqueeze(1).to_broadcast(spread),
        op=MULT,
    )
    nc.vector.tensor_tensor(
        out=by_sin[:, :, 1, :],
        in0=u[:, :, 0, :],
        in1=neg_sin[:].unsqueeze(1).to_broadcast(spread),
        op=MULT,
    )
    rotated = work.tile([P, heads, HEAD_DIM], F32)
    nc.vector.tensor_tensor(
        out=rotated[:].rearrange("p h d -> p (h d)"),
        in0=by_cos[:].rearrange("p r d -> p (r d)"),
        in1=by_sin[:].rearrange("p h s d -> p (h s d)"),
        op=ADD,
    )
    sum_sq = small.tile([P, heads], F32)
    for h in range(heads):
        squares = work.tile([P, HEAD_DIM], F32)
        nc.scalar.activation(
            out=squares[:], in_=rotated[:, h, :], func=SQUARE, accum_out=sum_sq[:, h : h + 1]
        )
    inv_rms = small.tile([P, heads], F32)
    nc.scalar.activation(
        out=inv_rms[:], in_=sum_sq[:], func=INV_SQRT, scale=1.0 / HEAD_DIM, bias=eps[:]
    )
    result = result_pool.tile([P, heads, HEAD_DIM], F32)
    for h in range(heads):
        nc.scalar.activation(
            out=result[:, h, :], in_=rotated[:, h, :], func=COPY, scale=inv_rms[:, h : h + 1]
        )
    nc.sync.dma_start(out=out_cols, in_=result[:].rearrange("p h d -> p (h d)"))


def finish_projection(nc, work, small, result_pool, acc, tables, out, last_bank_pieces):
    out_rows = out.rearrange("b t h d -> (b t) (h d)")
    for bank in range(BANKS):
        pieces = last_bank_pieces if bank == BANKS - 1 else 1
        piece_cols = BANK_COLS // pieces
        for piece in range(pieces):
            first = piece * piece_cols
            finish_heads(
                nc,
                work,
                small,
                result_pool,
                acc[bank][:, first : first + piece_cols],
                tables,
                out_rows[:, bank * BANK_COLS + first : bank * BANK_COLS + first + piece_cols],
            )


def tile_selfattention_pa_k_kernel(
    tc, x, wq_words, wq_scales, wk_words, wk_scales, cos, sin, out_0, out_1
):
    nc = tc.nc
    x_rows = x.flatten_outer_dims()
    with ExitStack() as ctx:
        ctx.enter_context(tc.manual_schedule())
        const = ctx.enter_context(tc.tile_pool(name="const", bufs=1))
        x_pool = ctx.enter_context(tc.tile_pool(name="x_pool", bufs=X_CHUNKS))
        word_pool = ctx.enter_context(tc.tile_pool(name="word_pool", bufs=LOADS))
        work = ctx.enter_context(tc.tile_pool(name="work", bufs=2))
        small = ctx.enter_context(tc.tile_pool(name="small", bufs=2))
        result_pool = ctx.enter_context(tc.tile_pool(name="result_pool", bufs=2 * BANKS - 1 + LAST_PIECES))
        psum = ctx.enter_context(tc.psum_pool(name="psum", bufs=8))

        identity = const.tile([P, P], F32)
        make_identity(nc, identity[:])
        cos_sb = const.tile([P, HALF], BF16)
        sin_sb = const.tile([P, HALF], BF16)
        nc.scalar.dma_start(out=cos_sb[:], in_=cos.flatten_outer_dims())
        nc.scalar.dma_start(out=sin_sb[:], in_=sin.flatten_outer_dims())
        x_codes = const.tile([P, GROUPS, TOKENS], U32, align_bytes=64)
        x_scales = const.tile([P, GROUPS, TOKENS], U8, align_bytes=64)
        q_planes = [
            const.tile([P, RUN_GROUPS, N_OUT], U8, align_bytes=64, name="q_planes%d" % run)
            for run in range(RUNS)
        ]
        k_planes = [
            const.tile([P, RUN_GROUPS, N_OUT], U8, align_bytes=64, name="k_planes%d" % run)
            for run in range(RUNS)
        ]
        for run in range(RUNS):
            nc.vector.memset(q_planes[run][:].bitcast(I32), 0)
        nc.vector.memset(k_planes[0][:].bitcast(I32), 0)

        x_chunks = []
        for c in range(X_CHUNKS):
            x_chunk = x_pool.tile([P, CHUNK_COLS], BF16)
            nc.sync.dma_start(out=x_chunk[:], in_=x_rows[:, c * CHUNK_COLS : (c + 1) * CHUNK_COLS])
            x_chunks.append(x_chunk)
        for run in range(RUNS):
            load_scale_rows(nc, q_planes, wq_scales, run)
        load_scale_rows(nc, k_planes, wk_scales, 0)
        q_words = [load_words(nc, word_pool, wq_words, load) for load in range(LOADS)]

        grouped_chunks = []
        for c in range(X_CHUNKS):
            x_words = x_chunks[c][:].bitcast(F32)
            grouped = x_pool.tile([P, CHUNK_COLS], BF16, align_bytes=64)
            grouped_words = grouped[:].bitcast(F32).rearrange(
                "p (g r s) -> p g r s", g=CHUNK_GROUPS, s=2
            )
            for pair in range(CHUNK_GROUPS // 2):
                xt = psum.tile([P, 2, 2, TOKENS], F32, tag="bank")
                for i in range(2):
                    first = (2 * pair + i) * WORDS_PER_GROUP
                    for s in range(2):
                        nc.tensor.transpose(
                            xt[:, i, s, :],
                            x_words[:, first + s : first + WORDS_PER_GROUP : 2],
                            identity[:],
                        )
                copy_out = nc.vector.tensor_copy if pair == 0 else nc.scalar.copy
                copy_out(
                    out=grouped_words[:, 2 * pair : 2 * pair + 2],
                    in_=xt[:].rearrange("p g s r -> p g r s"),
                )
            grouped_chunks.append(grouped)
        for c in range(X_CHUNKS):
            groups = slice(c * CHUNK_GROUPS, (c + 1) * CHUNK_GROUPS)
            nc.vector.quantize_mx(
                out=x_codes[:, groups, :].rearrange("p g r -> p (g r)").bitcast(FP8X4),
                scales=x_scales[:, groups, :].rearrange("p g r -> p (g r)"),
                in_=grouped_chunks[c][:],
            )

        nc.vector.memset(k_planes[1][:].bitcast(I32), 0)
        neg_sin = const.tile([P, HALF], BF16)
        nc.vector.tensor_scalar_mul(out=neg_sin[:], in0=sin_sb[:], scalar1=-1.0)
        eps = const.tile([P, 1], F32)
        nc.vector.memset(eps[:], EPS)
        tables = (cos_sb, sin_sb, neg_sin, eps)

        q_acc = [psum.tile([P, BANK_COLS], F32, tag="bank", name="q_acc%d" % b) for b in range(BANKS)]
        k_acc = [psum.tile([P, BANK_COLS], F32, tag="bank", name="k_acc%d" % b) for b in range(BANKS)]
        k_words = []
        for load in range(LOADS):
            multiply_load(nc, q_acc, x_codes, x_scales, q_words[load], q_planes, load)
            if load < WIDE_LOADS:
                k_words.append(load_words(nc, word_pool, wk_words, load))
            else:
                if load == WIDE_LOADS:
                    load_scale_rows(nc, k_planes, wk_scales, 1)
                k_words.append(load_tail_words(nc, word_pool, wk_words, load - WIDE_LOADS))

        finish_projection(nc, work, small, result_pool, q_acc, tables, out_0, 1)
        for load in range(WIDE_LOADS):
            multiply_load(nc, k_acc, x_codes, x_scales, k_words[load], k_planes, load)
        for bank in range(BANKS):
            multiply_tail(nc, k_acc, x_codes, x_scales, k_words[WIDE_LOADS + bank], k_planes, bank)
        finish_projection(nc, work, small, result_pool, k_acc, tables, out_1, LAST_PIECES)
